import numpy as np
import ml_dtypes


def mxq(x, axis, fmt="e4m3"):
    dtype, down = {"e4m3": (ml_dtypes.float8_e4m3fn, 7), "e5m2": (ml_dtypes.float8_e5m2, 14)}[fmt]
    v = np.moveaxis(np.asarray(x, np.float32).astype(ml_dtypes.bfloat16).astype(np.float64), axis, -1)
    blocks = v.reshape(v.shape[:-1] + (-1, 32))
    amax = np.abs(blocks).max(-1, keepdims=True)
    byte = np.maximum(np.where(amax > 0, np.frexp(amax)[1] - 1 + 127, 0) - down, 1)
    scale = np.exp2(byte - 127.0)
    codes = (blocks / scale).astype(np.float32).astype(dtype).astype(np.float64)
    return np.moveaxis((codes * scale).reshape(v.shape), -1, axis)


WIDE = False


def mx_kscale(k):
    if not WIDE:
        return np.ones(k)
    levels = np.array([10, -10, 5, -5, 0])
    a = np.random.permutation(np.resize(levels, k // 512 * 4)).reshape(k // 512, 4)
    idx = np.arange(k)
    return np.exp2(a[idx // 512, idx % 128 // 32])


BF16 = ml_dtypes.bfloat16


def bf(x):
    return np.asarray(x, np.float32).astype(BF16)


def f64(x):
    return np.asarray(x).astype(np.float64)


M, K, N = 16384, 512, 128


def ternary_quantize(w):
    thresh = 0.5 * np.abs(w).mean()
    return (w > thresh).astype(np.float64) - (w < -thresh).astype(np.float64)


def setup_inputs():
    s = mx_kscale(K)
    x = bf(np.random.standard_normal((M, K)) * s)
    weight = bf(np.random.uniform(-1.0, 1.0, (N, K)) / np.sqrt(K) / s)
    aw = np.abs(f64(weight))
    act = (aw > 0.5 * aw.mean()).mean(axis=0)
    c = 2.0 ** np.round(0.5 * np.log2((act * s * s).sum() / (0.75 * K)))
    return {"x": x,
            "weight": weight,
            "bias": bf(np.random.standard_normal(N) * 0.5 * np.sqrt(K) * c),
            "gamma": bf((1.0 + 0.1 * np.random.standard_normal(1)) / np.sqrt(K) / c)}


def reference(x, weight, bias, gamma):
    x = f64(x)
    weight = f64(weight)
    w_q = ternary_quantize(weight)
    w_ste = weight + (w_q - weight)
    out = (mxq(x, 1, "e4m3") @ mxq(w_ste, 1, "e4m3").T) + f64(bias)
    return out * f64(gamma)

@@ -1,0 +1,202 @@
+from contextlib import ExitStack
+
+import concourse.masks as masks
+import concourse.mybir as mybir
+
+F32 = mybir.dt.float32
+BF16 = mybir.dt.bfloat16
+U32 = mybir.dt.uint32
+U8 = mybir.dt.uint8
+FP8X4 = mybir.dt.float8_e4m3fn_x4
+ALU = mybir.AluOpType
+ACT = mybir.ActivationFunctionType
+
+P = 128
+M, K, N = 16384, 512, 128
+FLOPS = 2 * M * K * N
+UNIT = 4
+GROUP = 8
+CHUNK_T = [4, 4, 8, 16, 16, 16, 16, 16, 16, 16]
+SCALAR_GAMMA = (1, 3)
+
+
+def tile_ternarylineartorch_t_kernel(tc, x, weight, bias, gamma, out):
+    nc = tc.nc
+    assert sum(CHUNK_T) * P == M
+
+    units = []
+    groups = []
+    bases = []
+    base = 0
+    for c, t_c in enumerate(CHUNK_T):
+        bases.append(base)
+        base += t_c * P
+        for g0 in range(0, t_c, GROUP):
+            size = min(GROUP, t_c - g0)
+            groups.append((c, g0, size))
+            for t0 in range(g0, g0 + size, UNIT):
+                units.append((c, t0, len(groups) - 1, t0 - g0))
+    n_units = len(units)
+
+    with ExitStack() as ctx:
+        ctx.enter_context(tc.manual_schedule())
+        const = ctx.enter_context(tc.tile_pool(name="const", bufs=1))
+        xpool = ctx.enter_context(tc.tile_pool(name="xres", bufs=1))
+        opool = ctx.enter_context(tc.tile_pool(name="ores", bufs=1))
+        gpool = ctx.enter_context(tc.tile_pool(name="grp", bufs=3))
+        qpool = ctx.enter_context(tc.tile_pool(name="qnt", bufs=3))
+        ptp = ctx.enter_context(tc.psum_pool(name="ptp", bufs=4))
+        pop = ctx.enter_context(tc.psum_pool(name="pop", bufs=4))
+
+        brow = const.tile([P, 256], BF16, name="brow")
+        nc.vector.memset(brow[:], 0.0)
+        nc.scalar.dma_start(out=brow[0:1, 0:N], in_=bias.unsqueeze(0))
+        nc.scalar.dma_start(out=brow[0:1, N : N + 1], in_=gamma.unsqueeze(0))
+        ones_f = const.tile([P, P], F32, name="ones_f")
+        nc.vector.memset(ones_f[:], 1.0)
+        ones_b = const.tile([P, P], BF16, name="ones_b")
+        nc.vector.memset(ones_b[:], 1.0)
+        rowsum = const.tile([P, 2], F32, name="rowsum")
+        nc.vector.memset(rowsum[:], 0.0)
+        ident = const.tile([P, P], F32, name="ident")
+        masks.make_identity(nc, ident[:])
+
+        w_sb = const.tile([P, K], BF16, name="w_sb")
+        nc.sync.dma_start(out=w_sb[:], in_=weight)
+        x_f32 = []
+        for c, t_c in enumerate(CHUNK_T):
+            xt = xpool.tile([P, t_c * K], BF16, name="x%d" % c)
+            rows = x[bases[c] : bases[c] + t_c * P, :]
+            nc.sync.dma_start(out=xt[:], in_=rows.rearrange("(p t) k -> p (t k)", t=t_c))
+            x_f32.append(xt[:].bitcast(F32))
+
+        junk = const.tile([P, K], BF16, name="junk")
+        nc.scalar.activation(out=junk[:], in_=w_sb[:], func=ACT.Abs, accum_out=rowsum[:, 0:1])
+        w_f32 = w_sb[:].bitcast(F32)
+        ptw = ptp.tile([P, 2, 2, P], F32, name="ptw", tag="pt")
+        for u in range(2):
+            nc.tensor.transpose(ptw[:, 0, u, :], w_f32[:, P * u : P * (u + 1)], ident[:])
+        w_raw = const.tile([P, N * 4], BF16, name="w_raw")
+        nc.scalar.copy(
+            out=w_raw[:].bitcast(F32).rearrange("p (m u) -> p m u", u=2),
+            in_=ptw[:, 0, :, :].rearrange("p u m -> p m u"),
+        )
+        ps_tot = pop.tile([P, 512], F32, name="ps_tot", tag="po")
+        nc.tensor.matmul(out=ps_tot[:, 0:2], lhsT=ones_f[:], rhs=rowsum[:], start=True, stop=True)
+        thr = const.tile([P, 1], F32, name="thr")
+        nthr = const.tile([P, 1], F32, name="nthr")
+        half_mean = 0.5 / (N * K)
+        nc.vector.tensor_scalar(out=thr[:], in0=ps_tot[:, 0:1], scalar1=half_mean, scalar2=None, op0=ALU.mult)
+        nc.vector.tensor_scalar(out=nthr[:], in0=ps_tot[:, 0:1], scalar1=-half_mean, scalar2=None, op0=ALU.mult)
+        w_neg = const.tile([P, N * 4], BF16, name="w_neg")
+        nc.vector.tensor_scalar(out=w_neg[:], in0=w_raw[:], scalar1=nthr[:, 0:1], scalar2=None, op0=ALU.is_lt)
+        w_q = const.tile([P, N * 4], BF16, name="w_q", align_bytes=64)
+        nc.vector.scalar_tensor_tensor(
+            out=w_q[:], in0=w_raw[:], scalar=thr[:, 0:1], in1=w_neg[:], op0=ALU.is_gt, op1=ALU.subtract
+        )
+        w_codes = const.tile([P, N], U32, name="w_codes", align_bytes=64)
+        w_scl = const.tile([P, N], U8, name="w_scl", align_bytes=64)
+        nc.vector.quantize_mx(out=w_codes[:].bitcast(FP8X4), scales=w_scl[:], in_=w_q[:])
+
+        bias_bc = const.tile([P, UNIT * N], F32, name="bias_bc")
+        gamma_col = const.tile([P, 1], F32, name="gamma_col")
+
+        def spread_bias():
+            ps_b = pop.tile([P, 512], F32, name="ps_b", tag="po")
+            nc.tensor.matmul(out=ps_b[:, 0:256], lhsT=ones_b[:], rhs=brow[:], start=True, stop=True)
+            nc.vector.tensor_copy(
+                out=bias_bc[:].rearrange("p (r n) -> p r n", r=UNIT),
+                in_=ps_b[:, 0:N].unsqueeze(1).to_broadcast([P, UNIT, N]),
+            )
+            nc.vector.tensor_copy(out=gamma_col[:], in_=ps_b[:, N : N + 1])
+
+        pt_tiles = {}
+        g_tiles = {}
+        q_tiles = {}
+        po_tiles = {}
+        o_tiles = {}
+
+        def transposes(i):
+            c, t0 = units[i][0], units[i][1]
+            banks = []
+            for b in range(2):
+                pt = ptp.tile([P, 2, 2, P], F32, name="pt", tag="pt")
+                for j in range(2):
+                    for u in range(2):
+                        col = (t0 + 2 * b + j) * 256 + P * u
+                        nc.tensor.transpose(pt[:, j, u, :], x_f32[c][:, col : col + P], ident[:])
+                banks.append(pt)
+            pt_tiles[i] = banks
+
+        def exits(i):
+            g = gpool.tile([P, UNIT * P * 4], BF16, name="g", tag="g", align_bytes=64)
+            gf = g[:].bitcast(F32)
+            for b in range(2):
+                nc.scalar.copy(
+                    out=gf[:, 512 * b : 512 * (b + 1)].rearrange("p (j m u) -> p j m u", j=2, u=2),
+                    in_=pt_tiles[i][b][:].rearrange("p j u m -> p j m u"),
+                )
+            g_tiles[i] = g
+
+        def quantise(i):
+            codes = qpool.tile([P, UNIT * P], U32, name="codes", tag="codes", align_bytes=64)
+            scl = qpool.tile([P, UNIT * P], U8, name="scl", tag="scl", align_bytes=64)
+            nc.vector.quantize_mx(out=codes[:].bitcast(FP8X4), scales=scl[:], in_=g_tiles[i][:])
+            q_tiles[i] = (codes, scl)
+
+        def passes(i):
+            codes, scl = q_tiles[i]
+            po = pop.tile([P, 512], F32, name="po", tag="po")
+            for j in range(UNIT):
+                nc.tensor.matmul_mx(
+                    out=po[:, N * j : N * (j + 1)],
+                    lhsT=codes[:, P * j : P * (j + 1)].bitcast(FP8X4),
+                    lhsT_scale=scl[:, P * j : P * (j + 1)],
+                    rhs=w_codes[:].bitcast(FP8X4),
+                    rhs_scale=w_scl[:],
+                    start=True,
+                    stop=True,
+                )
+            po_tiles[i] = po
+
+        def o_slice(i):
+            gi, off = units[i][2], units[i][3]
+            return o_tiles[gi][:, off * N : (off + UNIT) * N]
+
+        def add_bias(i):
+            gi, off = units[i][2], units[i][3]
+            if off == 0:
+                o_tiles[gi] = opool.tile([P, groups[gi][2] * N], F32, name="o%d" % gi)
+            nc.vector.tensor_tensor(out=o_slice(i), in0=po_tiles[i][:], in1=bias_bc[:], op=ALU.add)
+
+        def times_gamma(i):
+            if i % 5 in SCALAR_GAMMA:
+                nc.scalar.activation(out=o_slice(i), in_=o_slice(i), func=ACT.Copy, scale=gamma_col[:, 0:1])
+            else:
+                nc.vector.tensor_scalar(
+                    out=o_slice(i), in0=o_slice(i), scalar1=gamma_col[:, 0:1], scalar2=None, op0=ALU.mult
+                )
+            gi, off = units[i][2], units[i][3]
+            c, g0, size = groups[gi]
+            if off + UNIT == size:
+                t_c = CHUNK_T[c]
+                rows = out[bases[c] : bases[c] + t_c * P, :].rearrange("(p t) o -> p t o", t=t_c)
+                nc.sync.dma_start(
+                    out=rows[:, g0 : g0 + size, :],
+                    in_=o_tiles[gi][:].rearrange("p (t o) -> p t o", o=N),
+                )
+
+        for i in range(n_units + 3):
+            if i < n_units:
+                transposes(i)
+                exits(i)
+            if 0 <= i - 1 < n_units:
+                quantise(i - 1)
+            if i == 2:
+                spread_bias()
+            if 0 <= i - 2 < n_units:
+                passes(i - 2)
+            if 0 <= i - 3 < n_units:
+                times_gamma(i - 3)
+            if 0 <= i - 2 < n_units:
+                add_bias(i - 2)

@@ -15,28 +15,36 @@ P = 128
 M, K, N = 16384, 512, 128
 FLOPS = 2 * M * K * N
 UNIT = 4
-GROUP = 8
-CHUNK_T = [4, 4, 8, 16, 16, 16, 16, 16, 16, 16]
+TPP = M // P
+LOAD_T = [4, 4, 4, 4, 8, 8, 16, 16, 16, 16, 16, 16]
+STORE_T = [32, 32, 16, 16, 8, 8, 8, 4, 4]
 SCALAR_GAMMA = (1, 3)
+SCALAR_TAIL = 5
 
 
 def tile_ternarylineartorch_t_kernel(tc, x, weight, bias, gamma, out):
     nc = tc.nc
-    assert sum(CHUNK_T) * P == M
+    assert sum(LOAD_T) == TPP and sum(STORE_T) == TPP
 
-    units = []
-    groups = []
-    bases = []
-    base = 0
-    for c, t_c in enumerate(CHUNK_T):
-        bases.append(base)
-        base += t_c * P
-        for g0 in range(0, t_c, GROUP):
-            size = min(GROUP, t_c - g0)
-            groups.append((c, g0, size))
-            for t0 in range(g0, g0 + size, UNIT):
-                units.append((c, t0, len(groups) - 1, t0 - g0))
-    n_units = len(units)
+    n_units = TPP // UNIT
+    load_of = []
+    load_start = []
+    t = 0
+    for c, t_c in enumerate(LOAD_T):
+        load_start.append(t)
+        t += t_c
+        for t0 in range(0, t_c, UNIT):
+            load_of.append((c, t0))
+    store_of = []
+    store_start = []
+    t = 0
+    for s, t_s in enumerate(STORE_T):
+        store_start.append(t)
+        t += t_s
+        for t0 in range(0, t_s, UNIT):
+            store_of.append((s, t0))
+    x_view = x.rearrange("(p t) k -> p t k", t=TPP)
+    out_view = out.rearrange("(p t) o -> p t o", t=TPP)
 
     with ExitStack() as ctx:
         ctx.enter_context(tc.manual_schedule())
@@ -64,10 +72,12 @@ def tile_ternarylineartorch_t_kernel(tc, x, weight, bias, gamma, out):
         w_sb = const.tile([P, K], BF16, name="w_sb")
         nc.sync.dma_start(out=w_sb[:], in_=weight)
         x_f32 = []
-        for c, t_c in enumerate(CHUNK_T):
+        for c, t_c in enumerate(LOAD_T):
             xt = xpool.tile([P, t_c * K], BF16, name="x%d" % c)
-            rows = x[bases[c] : bases[c] + t_c * P, :]
-            nc.sync.dma_start(out=xt[:], in_=rows.rearrange("(p t) k -> p (t k)", t=t_c))
+            nc.sync.dma_start(
+                out=xt[:].rearrange("p (t k) -> p t k", k=K),
+                in_=x_view[:, load_start[c] : load_start[c] + t_c, :],
+            )
             x_f32.append(xt[:].bitcast(F32))
 
         junk = const.tile([P, K], BF16, name="junk")
@@ -117,7 +127,7 @@ def tile_ternarylineartorch_t_kernel(tc, x, weight, bias, gamma, out):
         o_tiles = {}
 
         def transposes(i):
-            c, t0 = units[i][0], units[i][1]
+            c, t0 = load_of[i]
             banks = []
             for b in range(2):
                 pt = ptp.tile([P, 2, 2, P], F32, name="pt", tag="pt")
@@ -160,30 +170,31 @@ def tile_ternarylineartorch_t_kernel(tc, x, weight, bias, gamma, out):
             po_tiles[i] = po
 
         def o_slice(i):
-            gi, off = units[i][2], units[i][3]
-            return o_tiles[gi][:, off * N : (off + UNIT) * N]
+            s, off = store_of[i]
+            return o_tiles[s][:, off * N : (off + UNIT) * N]
 
         def add_bias(i):
-            gi, off = units[i][2], units[i][3]
+            s, off = store_of[i]
             if off == 0:
-                o_tiles[gi] = opool.tile([P, groups[gi][2] * N], F32, name="o%d" % gi)
+                o_tiles[s] = opool.tile([P, STORE_T[s] * N], F32, name="o%d" % s)
             nc.vector.tensor_tensor(out=o_slice(i), in0=po_tiles[i][:], in1=bias_bc[:], op=ALU.add)
 
         def times_gamma(i):
-            if i % 5 in SCALAR_GAMMA:
+            if i >= n_units - SCALAR_TAIL:
+                on_scalar = i < n_units - 1
+            else:
+                on_scalar = i % 5 in SCALAR_GAMMA
+            if on_scalar:
                 nc.scalar.activation(out=o_slice(i), in_=o_slice(i), func=ACT.Copy, scale=gamma_col[:, 0:1])
             else:
                 nc.vector.tensor_scalar(
                     out=o_slice(i), in0=o_slice(i), scalar1=gamma_col[:, 0:1], scalar2=None, op0=ALU.mult
                 )
-            gi, off = units[i][2], units[i][3]
-            c, g0, size = groups[gi]
-            if off + UNIT == size:
-                t_c = CHUNK_T[c]
-                rows = out[bases[c] : bases[c] + t_c * P, :].rearrange("(p t) o -> p t o", t=t_c)
+            s, off = store_of[i]
+            if off + UNIT == STORE_T[s]:
                 nc.sync.dma_start(
-                    out=rows[:, g0 : g0 + size, :],
-                    in_=o_tiles[gi][:].rearrange("p (t o) -> p t o", o=N),
+                    out=out_view[:, store_start[s] : store_start[s] + STORE_T[s], :],
+                    in_=o_tiles[s][:].rearrange("p (t o) -> p t o", o=N),
                 )
 
         for i in range(n_units + 3):

@@ -43,8 +43,8 @@ def tile_ternarylineartorch_t_kernel(tc, x, weight, bias, gamma, out):
         t += t_s
         for t0 in range(0, t_s, UNIT):
             store_of.append((s, t0))
-    x_view = x.rearrange("(p t) k -> p t k", t=TPP)
-    out_view = out.rearrange("(p t) o -> p t o", t=TPP)
+    x_view = x.rearrange("(p t) k -> p (t k)", t=TPP)
+    out_view = out.rearrange("(p t) o -> p (t o)", t=TPP)
 
     with ExitStack() as ctx:
         ctx.enter_context(tc.manual_schedule())
@@ -75,8 +75,8 @@ def tile_ternarylineartorch_t_kernel(tc, x, weight, bias, gamma, out):
         for c, t_c in enumerate(LOAD_T):
             xt = xpool.tile([P, t_c * K], BF16, name="x%d" % c)
             nc.sync.dma_start(
-                out=xt[:].rearrange("p (t k) -> p t k", k=K),
-                in_=x_view[:, load_start[c] : load_start[c] + t_c, :],
+                out=xt[:],
+                in_=x_view[:, load_start[c] * K : (load_start[c] + t_c) * K],
             )
             x_f32.append(xt[:].bitcast(F32))
 
@@ -193,8 +193,8 @@ def tile_ternarylineartorch_t_kernel(tc, x, weight, bias, gamma, out):
             s, off = store_of[i]
             if off + UNIT == STORE_T[s]:
                 nc.sync.dma_start(
-                    out=out_view[:, store_start[s] : store_start[s] + STORE_T[s], :],
-                    in_=o_tiles[s][:].rearrange("p (t o) -> p t o", o=N),
+                    out=out_view[:, store_start[s] * N : (store_start[s] + STORE_T[s]) * N],
+                    in_=o_tiles[s][:],
                 )
 
         for i in range(n_units + 3):

@@ -16,8 +16,8 @@ M, K, N = 16384, 512, 128
 FLOPS = 2 * M * K * N
 UNIT = 4
 TPP = M // P
-LOAD_T = [4, 4, 4, 4, 8, 8, 16, 16, 16, 16, 16, 16]
-STORE_T = [32, 32, 16, 16, 8, 8, 8, 4, 4]
+LOAD_T = [4, 4, 4, 4, 8, 8, 8, 8, 12, 16, 16, 16, 20]
+STORE_T = [64, 32, 20, 12]
 SCALAR_GAMMA = (1, 3)
 SCALAR_TAIL = 5
 
@@ -58,14 +58,14 @@ def tile_ternarylineartorch_t_kernel(tc, x, weight, bias, gamma, out):
 
         brow = const.tile([P, 256], BF16, name="brow")
         nc.vector.memset(brow[:], 0.0)
-        nc.scalar.dma_start(out=brow[0:1, 0:N], in_=bias.unsqueeze(0))
-        nc.scalar.dma_start(out=brow[0:1, N : N + 1], in_=gamma.unsqueeze(0))
+        rowsum = const.tile([P, 2], F32, name="rowsum")
+        nc.vector.memset(rowsum[:], 0.0)
+        early = const.tile([P, 1], F32, name="early")
+        nc.scalar.activation(out=early[:], in_=rowsum[:, 1:2], func=ACT.Abs)
         ones_f = const.tile([P, P], F32, name="ones_f")
         nc.vector.memset(ones_f[:], 1.0)
         ones_b = const.tile([P, P], BF16, name="ones_b")
         nc.vector.memset(ones_b[:], 1.0)
-        rowsum = const.tile([P, 2], F32, name="rowsum")
-        nc.vector.memset(rowsum[:], 0.0)
         ident = const.tile([P, P], F32, name="ident")
         masks.make_identity(nc, ident[:])
 
@@ -73,6 +73,9 @@ def tile_ternarylineartorch_t_kernel(tc, x, weight, bias, gamma, out):
         nc.sync.dma_start(out=w_sb[:], in_=weight)
         x_f32 = []
         for c, t_c in enumerate(LOAD_T):
+            if c == 1:
+                nc.sync.dma_start(out=brow[0:1, 0:N], in_=bias.unsqueeze(0))
+                nc.sync.dma_start(out=brow[0:1, N : N + 1], in_=gamma.unsqueeze(0))
             xt = xpool.tile([P, t_c * K], BF16, name="x%d" % c)
             nc.sync.dma_start(
                 out=xt[:],

from contextlib import ExitStack

import concourse.masks as masks
import concourse.mybir as mybir

F32 = mybir.dt.float32
BF16 = mybir.dt.bfloat16
U32 = mybir.dt.uint32
U8 = mybir.dt.uint8
FP8X4 = mybir.dt.float8_e4m3fn_x4
ALU = mybir.AluOpType
ACT = mybir.ActivationFunctionType

P = 128
M, K, N = 16384, 512, 128
FLOPS = 2 * M * K * N
UNIT = 4
TPP = M // P
LOAD_T = [4, 4, 4, 4, 8, 8, 8, 8, 12, 16, 16, 16, 20]
STORE_T = [64, 32, 20, 12]
SCALAR_GAMMA = (1, 3)
SCALAR_TAIL = 5


def tile_ternarylineartorch_t_kernel(tc, x, weight, bias, gamma, out):
    nc = tc.nc
    assert sum(LOAD_T) == TPP and sum(STORE_T) == TPP

    n_units = TPP // UNIT
    load_of = []
    load_start = []
    t = 0
    for c, t_c in enumerate(LOAD_T):
        load_start.append(t)
        t += t_c
        for t0 in range(0, t_c, UNIT):
            load_of.append((c, t0))
    store_of = []
    store_start = []
    t = 0
    for s, t_s in enumerate(STORE_T):
        store_start.append(t)
        t += t_s
        for t0 in range(0, t_s, UNIT):
            store_of.append((s, t0))
    x_view = x.rearrange("(p t) k -> p (t k)", t=TPP)
    out_view = out.rearrange("(p t) o -> p (t o)", t=TPP)

    with ExitStack() as ctx:
        ctx.enter_context(tc.manual_schedule())
        const = ctx.enter_context(tc.tile_pool(name="const", bufs=1))
        xpool = ctx.enter_context(tc.tile_pool(name="xres", bufs=1))
        opool = ctx.enter_context(tc.tile_pool(name="ores", bufs=1))
        gpool = ctx.enter_context(tc.tile_pool(name="grp", bufs=3))
        qpool = ctx.enter_context(tc.tile_pool(name="qnt", bufs=3))
        ptp = ctx.enter_context(tc.psum_pool(name="ptp", bufs=4))
        pop = ctx.enter_context(tc.psum_pool(name="pop", bufs=4))

        brow = const.tile([P, 256], BF16, name="brow")
        nc.vector.memset(brow[:], 0.0)
        rowsum = const.tile([P, 2], F32, name="rowsum")
        nc.vector.memset(rowsum[:], 0.0)
        early = const.tile([P, 1], F32, name="early")
        nc.scalar.activation(out=early[:], in_=rowsum[:, 1:2], func=ACT.Abs)
        ones_f = const.tile([P, P], F32, name="ones_f")
        nc.vector.memset(ones_f[:], 1.0)
        ones_b = const.tile([P, P], BF16, name="ones_b")
        nc.vector.memset(ones_b[:], 1.0)
        ident = const.tile([P, P], F32, name="ident")
        masks.make_identity(nc, ident[:])

        w_sb = const.tile([P, K], BF16, name="w_sb")
        nc.sync.dma_start(out=w_sb[:], in_=weight)
        x_f32 = []
        for c, t_c in enumerate(LOAD_T):
            if c == 1:
                nc.sync.dma_start(out=brow[0:1, 0:N], in_=bias.unsqueeze(0))
                nc.sync.dma_start(out=brow[0:1, N : N + 1], in_=gamma.unsqueeze(0))
            xt = xpool.tile([P, t_c * K], BF16, name="x%d" % c)
            nc.sync.dma_start(
                out=xt[:],
                in_=x_view[:, load_start[c] * K : (load_start[c] + t_c) * K],
            )
            x_f32.append(xt[:].bitcast(F32))

        junk = const.tile([P, K], BF16, name="junk")
        nc.scalar.activation(out=junk[:], in_=w_sb[:], func=ACT.Abs, accum_out=rowsum[:, 0:1])
        w_f32 = w_sb[:].bitcast(F32)
        ptw = ptp.tile([P, 2, 2, P], F32, name="ptw", tag="pt")
        for u in range(2):
            nc.tensor.transpose(ptw[:, 0, u, :], w_f32[:, P * u : P * (u + 1)], ident[:])
        w_raw = const.tile([P, N * 4], BF16, name="w_raw")
        nc.scalar.copy(
            out=w_raw[:].bitcast(F32).rearrange("p (m u) -> p m u", u=2),
            in_=ptw[:, 0, :, :].rearrange("p u m -> p m u"),
        )
        ps_tot = pop.tile([P, 512], F32, name="ps_tot", tag="po")
        nc.tensor.matmul(out=ps_tot[:, 0:2], lhsT=ones_f[:], rhs=rowsum[:], start=True, stop=True)
        thr = const.tile([P, 1], F32, name="thr")
        nthr = const.tile([P, 1], F32, name="nthr")
        half_mean = 0.5 / (N * K)
        nc.vector.tensor_scalar(out=thr[:], in0=ps_tot[:, 0:1], scalar1=half_mean, scalar2=None, op0=ALU.mult)
        nc.vector.tensor_scalar(out=nthr[:], in0=ps_tot[:, 0:1], scalar1=-half_mean, scalar2=None, op0=ALU.mult)
        w_neg = const.tile([P, N * 4], BF16, name="w_neg")
        nc.vector.tensor_scalar(out=w_neg[:], in0=w_raw[:], scalar1=nthr[:, 0:1], scalar2=None, op0=ALU.is_lt)
        w_q = const.tile([P, N * 4], BF16, name="w_q", align_bytes=64)
        nc.vector.scalar_tensor_tensor(
            out=w_q[:], in0=w_raw[:], scalar=thr[:, 0:1], in1=w_neg[:], op0=ALU.is_gt, op1=ALU.subtract
        )
        w_codes = const.tile([P, N], U32, name="w_codes", align_bytes=64)
        w_scl = const.tile([P, N], U8, name="w_scl", align_bytes=64)
        nc.vector.quantize_mx(out=w_codes[:].bitcast(FP8X4), scales=w_scl[:], in_=w_q[:])

        bias_bc = const.tile([P, UNIT * N], F32, name="bias_bc")
        gamma_col = const.tile([P, 1], F32, name="gamma_col")

        def spread_bias():
            ps_b = pop.tile([P, 512], F32, name="ps_b", tag="po")
            nc.tensor.matmul(out=ps_b[:, 0:256], lhsT=ones_b[:], rhs=brow[:], start=True, stop=True)
            nc.vector.tensor_copy(
                out=bias_bc[:].rearrange("p (r n) -> p r n", r=UNIT),
                in_=ps_b[:, 0:N].unsqueeze(1).to_broadcast([P, UNIT, N]),
            )
            nc.vector.tensor_copy(out=gamma_col[:], in_=ps_b[:, N : N + 1])

        pt_tiles = {}
        g_tiles = {}
        q_tiles = {}
        po_tiles = {}
        o_tiles = {}

        def transposes(i):
            c, t0 = load_of[i]
            banks = []
            for b in range(2):
                pt = ptp.tile([P, 2, 2, P], F32, name="pt", tag="pt")
                for j in range(2):
                    for u in range(2):
                        col = (t0 + 2 * b + j) * 256 + P * u
                        nc.tensor.transpose(pt[:, j, u, :], x_f32[c][:, col : col + P], ident[:])
                banks.append(pt)
            pt_tiles[i] = banks

        def exits(i):
            g = gpool.tile([P, UNIT * P * 4], BF16, name="g", tag="g", align_bytes=64)
            gf = g[:].bitcast(F32)
            for b in range(2):
                nc.scalar.copy(
                    out=gf[:, 512 * b : 512 * (b + 1)].rearrange("p (j m u) -> p j m u", j=2, u=2),
                    in_=pt_tiles[i][b][:].rearrange("p j u m -> p j m u"),
                )
            g_tiles[i] = g

        def quantise(i):
            codes = qpool.tile([P, UNIT * P], U32, name="codes", tag="codes", align_bytes=64)
            scl = qpool.tile([P, UNIT * P], U8, name="scl", tag="scl", align_bytes=64)
            nc.vector.quantize_mx(out=codes[:].bitcast(FP8X4), scales=scl[:], in_=g_tiles[i][:])
            q_tiles[i] = (codes, scl)

        def passes(i):
            codes, scl = q_tiles[i]
            po = pop.tile([P, 512], F32, name="po", tag="po")
            for j in range(UNIT):
                nc.tensor.matmul_mx(
                    out=po[:, N * j : N * (j + 1)],
                    lhsT=codes[:, P * j : P * (j + 1)].bitcast(FP8X4),
                    lhsT_scale=scl[:, P * j : P * (j + 1)],
                    rhs=w_codes[:].bitcast(FP8X4),
                    rhs_scale=w_scl[:],
                    start=True,
                    stop=True,
                )
            po_tiles[i] = po

        def o_slice(i):
            s, off = store_of[i]
            return o_tiles[s][:, off * N : (off + UNIT) * N]

        def add_bias(i):
            s, off = store_of[i]
            if off == 0:
                o_tiles[s] = opool.tile([P, STORE_T[s] * N], F32, name="o%d" % s)
            nc.vector.tensor_tensor(out=o_slice(i), in0=po_tiles[i][:], in1=bias_bc[:], op=ALU.add)

        def times_gamma(i):
            if i >= n_units - SCALAR_TAIL:
                on_scalar = i < n_units - 1
            else:
                on_scalar = i % 5 in SCALAR_GAMMA
            if on_scalar:
                nc.scalar.activation(out=o_slice(i), in_=o_slice(i), func=ACT.Copy, scale=gamma_col[:, 0:1])
            else:
                nc.vector.tensor_scalar(
                    out=o_slice(i), in0=o_slice(i), scalar1=gamma_col[:, 0:1], scalar2=None, op0=ALU.mult
                )
            s, off = store_of[i]
            if off + UNIT == STORE_T[s]:
                nc.sync.dma_start(
                    out=out_view[:, store_start[s] * N : (store_start[s] + STORE_T[s]) * N],
                    in_=o_tiles[s][:],
                )

        for i in range(n_units + 3):
            if i < n_units:
                transposes(i)
                exits(i)
            if 0 <= i - 1 < n_units:
                quantise(i - 1)
            if i == 2:
                spread_bias()
            if 0 <= i - 2 < n_units:
                passes(i - 2)
            if 0 <= i - 3 < n_units:
                times_gamma(i - 3)
            if 0 <= i - 2 < n_units:
                add_bias(i - 2)
